import numpy as np
import ml_dtypes


def mxq(x, axis, fmt="e4m3"):
    dtype, down = {"e4m3": (ml_dtypes.float8_e4m3fn, 7), "e5m2": (ml_dtypes.float8_e5m2, 14)}[fmt]
    v = np.moveaxis(np.asarray(x, np.float32).astype(ml_dtypes.bfloat16).astype(np.float64), axis, -1)
    blocks = v.reshape(v.shape[:-1] + (-1, 32))
    amax = np.abs(blocks).max(-1, keepdims=True)
    byte = np.maximum(np.where(amax > 0, np.frexp(amax)[1] - 1 + 127, 0) - down, 1)
    scale = np.exp2(byte - 127.0)
    codes = (blocks / scale).astype(np.float32).astype(dtype).astype(np.float64)
    return np.moveaxis((codes * scale).reshape(v.shape), -1, axis)


WIDE = False


def mx_kscale(k):
    if not WIDE:
        return np.ones(k)
    levels = np.array([10, -10, 5, -5, 0])
    a = np.random.permutation(np.resize(levels, k // 512 * 4)).reshape(k // 512, 4)
    idx = np.arange(k)
    return np.exp2(a[idx // 512, idx % 128 // 32])


BF16 = ml_dtypes.bfloat16


def bf(x):
    return np.asarray(x, np.float32).astype(BF16)


def f64(x):
    return np.asarray(x).astype(np.float64)


B, HP, WP, E, F, NH, WS = 4, 32, 80, 512, 512, 16, 8
NWH, NWW = HP // WS, WP // WS
L, N = B * NWH * NWW, WS * WS
LN_EPS = 1e-5
ERF_TERMS = 100


def erf(z):
    z = np.clip(z, -6.0, 6.0)
    u = z * z
    c = np.cumprod(np.concatenate([[1.0], 2.0 / (2.0 * np.arange(1, ERF_TERMS) + 1.0)]))
    acc = np.full_like(u, c[-1])
    for cn in c[-2::-1]:
        acc *= u
        acc += cn
    return 2.0 / np.sqrt(np.pi) * z * np.exp(-u) * acc


def gelu(v):
    return 0.5 * v * (1.0 + erf(v / np.sqrt(2.0)))


def layernorm(x, g, b):
    mu = x.mean(-1, keepdims=True)
    var = ((x - mu) ** 2).mean(-1, keepdims=True)
    return (x - mu) / np.sqrt(var + LN_EPS) * g + b


def setup_inputs():
    s = mx_kscale(E)
    s = s / s.max()
    return {"y": bf(np.random.standard_normal((L, N, E)) * s),
            "w1": bf(np.random.standard_normal((F, E)) / np.sqrt(E) / s),
            "b1": bf(np.random.standard_normal(F) * 0.2),
            "w2": bf(np.random.standard_normal((E, F)) * 1.5 / np.sqrt(F)),
            "b2": bf(np.random.standard_normal(E) * 0.2),
            "ln2_g": bf(1.0 + 0.1 * np.random.standard_normal(E)),
            "ln2_b": bf(np.random.standard_normal(E) * 0.2)}


def reference(y, w1, b1, w2, b2, ln2_g, ln2_b):
    y = f64(y)
    h = gelu((mxq(y, 2, "e4m3") @ mxq(f64(w1), 1, "e4m3").T) + f64(b1))
    ffn = (mxq(h, 2, "e4m3") @ mxq(f64(w2), 1, "e4m3").T) + f64(b2)
    z = layernorm(y + ffn, f64(ln2_g), f64(ln2_b))
    z = z.reshape(B, NWH, NWW, WS, WS, E).transpose(0, 1, 3, 2, 4, 5)
    return z.reshape(B, HP * WP, E)

@@ -1,0 +1,258 @@
+from contextlib import ExitStack
+
+import concourse.mybir as mybir
+from concourse.masks import make_identity
+
+F32 = mybir.dt.float32
+BF16 = mybir.dt.bfloat16
+U32 = mybir.dt.uint32
+U8 = mybir.dt.uint8
+FP8X4 = mybir.dt.float8_e4m3fn_x4
+ACT = mybir.ActivationFunctionType
+ALU = mybir.AluOpType
+
+P = 128
+PACK = 4
+CH = P * PACK
+WORDS = CH // 2
+IMAGES, WIN_ROWS, WIN_COLS, WS = 4, 4, 10, 8
+BLOCKS = 4
+GROUP = BLOCKS * P
+GROUPS_IN_SLAB = WS // BLOCKS
+N_GROUPS = WIN_COLS * GROUPS_IN_SLAB
+LN_EPS = 1e-5
+FLOPS = 2 * 2 * IMAGES * WIN_ROWS * WIN_COLS * WS * WS * CH * CH
+
+
+def tile_swintransformerblock_pb_t_kernel(tc, y, w1, b1, w2, b2, ln2_g, ln2_b, out):
+    nc = tc.nc
+    y_slabs = y.rearrange("(iw ww) (r c) e -> ww r iw (c e)", ww=WIN_COLS, c=WS)
+    out_slabs = out.rearrange("i (wr r ww c) e -> ww (i wr r) (c e)", wr=WIN_ROWS, r=WS, ww=WIN_COLS, c=WS)
+
+    with ExitStack() as ctx:
+        const = ctx.enter_context(tc.tile_pool(name="const", bufs=1))
+        slabs = ctx.enter_context(tc.tile_pool(name="slabs", bufs=3))
+        work = ctx.enter_context(tc.tile_pool(name="work", bufs=2))
+        results = ctx.enter_context(tc.tile_pool(name="results", bufs=3))
+        psum_flip = ctx.enter_context(tc.psum_pool(name="psum_flip", bufs=2))
+        psum_hid = ctx.enter_context(tc.psum_pool(name="psum_hid", bufs=PACK))
+        psum_ffn = ctx.enter_context(tc.psum_pool(name="psum_ffn", bufs=2))
+        ctx.enter_context(tc.manual_schedule())
+
+        def load_slab(ww):
+            y_sb = slabs.tile([P, WS * CH], BF16)
+            for r in range(WS):
+                nc.sync.dma_start(out=y_sb[r:P:WS, :], in_=y_slabs[ww, r])
+            return y_sb
+
+        def flip_rows(words):
+            banks = []
+            for pair in range(BLOCKS // 2):
+                flipped = psum_flip.tile([P, 2, 2, P], F32)
+                for j in range(2):
+                    for u in range(2):
+                        first = ((2 * pair + j) * 2 + u) * P
+                        nc.tensor.transpose(flipped[:, j, u, :], words[:, first : first + P], ident[:])
+                banks.append(flipped)
+            return banks
+
+        def collect_flipped(banks):
+            grouped = work.tile([P, GROUP, PACK], BF16, align_bytes=64)
+            grouped_words = grouped[:].bitcast(F32)
+            for pair in range(BLOCKS // 2):
+                nc.scalar.copy(
+                    out=grouped_words[:, 2 * pair * P : 2 * (pair + 1) * P, :].rearrange("p (j r) u -> p j r u", j=2),
+                    in_=banks[pair][:].rearrange("p j u r -> p j r u"),
+                )
+            return grouped
+
+        def quantise(pool, grouped, label):
+            codes = pool.tile([P, GROUP], U32, align_bytes=64, name=label + "_codes")
+            scales = pool.tile([P, GROUP], U8, align_bytes=64, name=label + "_scales")
+            nc.vector.quantize_mx(
+                out=codes[:].bitcast(FP8X4), scales=scales[:], in_=grouped[:].rearrange("p r t -> p (r t)")
+            )
+            return codes, scales
+
+        ident = const.tile([P, P], F32)
+        make_identity(nc, ident[:])
+        minus_half = const.tile([P, BLOCKS], F32)
+        nc.vector.memset(minus_half[:], -0.5)
+
+        b1_bf = const.tile([P, PACK], BF16)
+        nc.sync.dma_start(
+            out=b1_bf[:].rearrange("m (u e) -> m u e", u=2), in_=b1.rearrange("(u m e) -> m u e", u=2, e=2)
+        )
+        w1_sb = const.tile([P, PACK * CH], BF16)
+        nc.sync.dma_start(
+            out=w1_sb[:].rearrange("m (u x) -> m u x", u=2), in_=w1.rearrange("(u m e) k -> m u (e k)", u=2, e=2)
+        )
+        y_of_slab = {0: load_slab(0)}
+        w2_sb = const.tile([P, PACK * CH], BF16)
+        nc.sync.dma_start(
+            out=w2_sb[:].rearrange("m (j f) -> m j f", j=PACK), in_=w2.rearrange("(j m) f -> m j f", m=P)
+        )
+        b2_all = const.tile([P, CH], BF16)
+        nc.sync.dma_start(out=b2_all[:], in_=b2.partition_broadcast(P))
+        gain_all = const.tile([P, CH], BF16)
+        nc.sync.dma_start(out=gain_all[:], in_=ln2_g.partition_broadcast(P))
+        shift_all = const.tile([P, CH], BF16)
+        nc.sync.dma_start(out=shift_all[:], in_=ln2_b.partition_broadcast(P))
+
+        b1_col = const.tile([P, PACK], F32)
+        nc.vector.tensor_copy(out=b1_col[:], in_=b1_bf[:])
+        w1_codes, w1_scales = quantise(const, collect_flipped(flip_rows(w1_sb[:].bitcast(F32))), "w1")
+        w2_codes, w2_scales = quantise(const, collect_flipped(flip_rows(w2_sb[:].bitcast(F32))), "w2")
+
+        y_flipped, y_mx, hid_banks, h_mx, y_plus_b2, resid, neg_mean, rstd, normed = {}, {}, {}, {}, {}, {}, {}, {}, {}
+
+        def flip_tokens(g):
+            words = y_of_slab[g // GROUPS_IN_SLAB][:].bitcast(F32)
+            first = (g % GROUPS_IN_SLAB) * BLOCKS * WORDS
+            y_flipped[g] = flip_rows(words[:, first : first + BLOCKS * WORDS])
+
+        def add_second_bias(g):
+            y_sb = y_of_slab[g // GROUPS_IN_SLAB]
+            total = work.tile([P, BLOCKS, CH], F32, name="y_plus_b2")
+            for s in range(BLOCKS):
+                c = (g % GROUPS_IN_SLAB) * BLOCKS + s
+                nc.gpsimd.tensor_tensor(out=total[:, s, :], in0=y_sb[:, c * CH : (c + 1) * CH], in1=b2_all[:], op=ALU.add)
+            y_plus_b2[g] = total
+
+        def first_matmul(g):
+            codes, scales = y_mx[g]
+            hid_banks[g] = []
+            for t in range(PACK):
+                cols = slice(t * P, (t + 1) * P)
+                acc = psum_hid.tile([P, GROUP], F32)
+                nc.tensor.matmul_mx(
+                    out=acc[:],
+                    lhsT=w1_codes[:, cols].bitcast(FP8X4),
+                    lhsT_scale=w1_scales[:, cols],
+                    rhs=codes[:].bitcast(FP8X4),
+                    rhs_scale=scales[:],
+                    start=True,
+                    stop=True,
+                )
+                hid_banks[g].append(acc)
+
+        def gelu(g):
+            hidden = work.tile([P, PACK, GROUP], BF16)
+            for t in range(PACK):
+                nc.scalar.activation(
+                    out=hidden[:, t, :], in_=hid_banks[g][t][:], func=ACT.Gelu, bias=b1_col[:, t : t + 1], scale=1.0
+                )
+            return hidden
+
+        def regroup(hidden):
+            grouped = work.tile([P, GROUP, PACK], BF16, align_bytes=64, name="h_grouped")
+            nc.scalar.copy(
+                out=grouped[:].rearrange("p (c i) t -> p c t i", i=4),
+                in_=hidden[:].rearrange("p t (c i) -> p c t i", i=4),
+            )
+            return grouped
+
+        def second_matmul(g):
+            codes, scales = h_mx[g]
+            total = work.tile([P, BLOCKS, CH], F32, name="resid")
+            row_sum = work.tile([P, BLOCKS], F32)
+            for s in range(BLOCKS):
+                cols = slice(s * P, (s + 1) * P)
+                acc = psum_ffn.tile([P, CH], F32)
+                nc.tensor.matmul_mx(
+                    out=acc[:],
+                    lhsT=codes[:, cols].bitcast(FP8X4),
+                    lhsT_scale=scales[:, cols],
+                    rhs=w2_codes[:].bitcast(FP8X4),
+                    rhs_scale=w2_scales[:],
+                    start=True,
+                    stop=True,
+                )
+                nc.vector.scalar_tensor_tensor(
+                    out=total[:, s, :],
+                    in0=acc[:],
+                    scalar=1.0,
+                    in1=y_plus_b2[g][:, s, :],
+                    op0=ALU.mult,
+                    op1=ALU.add,
+                    accum_out=row_sum[:, s : s + 1],
+                )
+            minus_mean = work.tile([P, BLOCKS], F32)
+            nc.vector.tensor_scalar_mul(out=minus_mean[:], in0=row_sum[:], scalar1=-1.0 / CH)
+            resid[g], neg_mean[g] = total, minus_mean
+
+        def variance(g):
+            square_sum = work.tile([P, BLOCKS], F32)
+            for s in range(BLOCKS):
+                squares = work.tile([P, CH], F32)
+                nc.scalar.activation(
+                    out=squares[:],
+                    in_=resid[g][:, s, :],
+                    func=ACT.Square,
+                    bias=neg_mean[g][:, s : s + 1],
+                    scale=1.0,
+                    accum_out=square_sum[:, s : s + 1],
+                )
+            var_eps = work.tile([P, BLOCKS], F32)
+            nc.gpsimd.tensor_scalar(
+                out=var_eps[:], in0=square_sum[:], scalar1=1.0 / CH, scalar2=LN_EPS, op0=ALU.mult, op1=ALU.add
+            )
+            inv_std = work.tile([P, BLOCKS], F32)
+            nc.gpsimd.tensor_tensor(out=inv_std[:], in0=var_eps[:], in1=minus_half[:], op=ALU.pow)
+            rstd[g] = inv_std
+
+        def centre_and_gain(g):
+            scaled = results.tile([P, BLOCKS, CH], F32)
+            for s in range(BLOCKS):
+                nc.vector.scalar_tensor_tensor(
+                    out=scaled[:, s, :],
+                    in0=resid[g][:, s, :],
+                    scalar=neg_mean[g][:, s : s + 1],
+                    in1=gain_all[:],
+                    op0=ALU.add,
+                    op1=ALU.mult,
+                )
+            normed[g] = scaled
+
+        def scale_shift_store(g):
+            scaled = normed[g]
+            for s in range(BLOCKS):
+                nc.vector.scalar_tensor_tensor(
+                    out=scaled[:, s, :],
+                    in0=scaled[:, s, :],
+                    scalar=rstd[g][:, s : s + 1],
+                    in1=shift_all[:],
+                    op0=ALU.mult,
+                    op1=ALU.add,
+                )
+            first = (g % GROUPS_IN_SLAB) * BLOCKS * CH
+            nc.sync.dma_start(
+                out=out_slabs[g // GROUPS_IN_SLAB][:, first : first + BLOCKS * CH],
+                in_=scaled[:].rearrange("p s e -> p (s e)"),
+            )
+
+        def live(g):
+            return 0 <= g < N_GROUPS
+
+        for k in range(-3, N_GROUPS + 1):
+            if live(k + 1):
+                add_second_bias(k + 1)
+            if live(k):
+                second_matmul(k)
+            if live(k + 1):
+                hidden = gelu(k + 1)
+            if live(k + 2):
+                y_mx[k + 2] = quantise(work, collect_flipped(y_flipped[k + 2]), "y")
+                first_matmul(k + 2)
+            if live(k + 3):
+                if (k + 3) % GROUPS_IN_SLAB == 0 and live(k + 3 + GROUPS_IN_SLAB):
+                    ahead = (k + 3) // GROUPS_IN_SLAB + 1
+                    y_of_slab[ahead] = load_slab(ahead)
+                flip_tokens(k + 3)
+            if live(k - 1):
+                scale_shift_store(k - 1)
+            if live(k + 1):
+                h_mx[k + 1] = quantise(work, regroup(hidden), "h")
+            if live(k):
+                variance(k)
+                centre_and_gain(k)

@@ -35,8 +35,9 @@ def tile_swintransformerblock_pb_t_kernel(tc, y, w1, b1, w2, b2, ln2_g, ln2_b, o
         work = ctx.enter_context(tc.tile_pool(name="work", bufs=2))
         results = ctx.enter_context(tc.tile_pool(name="results", bufs=3))
         psum_flip = ctx.enter_context(tc.psum_pool(name="psum_flip", bufs=2))
-        psum_hid = ctx.enter_context(tc.psum_pool(name="psum_hid", bufs=PACK))
+        psum_hid = ctx.enter_context(tc.psum_pool(name="psum_hid", bufs=3))
         psum_ffn = ctx.enter_context(tc.psum_pool(name="psum_ffn", bufs=2))
+        psum_const = ctx.enter_context(tc.psum_pool(name="psum_const", bufs=1))
         ctx.enter_context(tc.manual_schedule())
 
         def load_slab(ww):
@@ -98,6 +99,12 @@ def tile_swintransformerblock_pb_t_kernel(tc, y, w1, b1, w2, b2, ln2_g, ln2_b, o
         nc.sync.dma_start(out=gain_all[:], in_=ln2_g.partition_broadcast(P))
         shift_all = const.tile([P, CH], BF16)
         nc.sync.dma_start(out=shift_all[:], in_=ln2_b.partition_broadcast(P))
+
+        ident_bf = const.tile([P, P], BF16)
+        make_identity(nc, ident_bf[:])
+        gain_shift = psum_const.tile([P, 2, CH], BF16)
+        nc.tensor.matmul(out=gain_shift[:, 0, :], lhsT=ident_bf[:], rhs=gain_all[:], start=True, stop=True)
+        nc.tensor.matmul(out=gain_shift[:, 1, :], lhsT=ident_bf[:], rhs=shift_all[:], start=True, stop=True)
 
         b1_col = const.tile([P, PACK], F32)
         nc.vector.tensor_copy(out=b1_col[:], in_=b1_bf[:])
@@ -208,7 +215,7 @@ def tile_swintransformerblock_pb_t_kernel(tc, y, w1, b1, w2, b2, ln2_g, ln2_b, o
                     out=scaled[:, s, :],
                     in0=resid[g][:, s, :],
                     scalar=neg_mean[g][:, s : s + 1],
-                    in1=gain_all[:],
+                    in1=gain_shift[:, 0, :],
                     op0=ALU.add,
                     op1=ALU.mult,
                 )
@@ -221,7 +228,7 @@ def tile_swintransformerblock_pb_t_kernel(tc, y, w1, b1, w2, b2, ln2_g, ln2_b, o
                     out=scaled[:, s, :],
                     in0=scaled[:, s, :],
                     scalar=rstd[g][:, s : s + 1],
-                    in1=shift_all[:],
+                    in1=gain_shift[:, 1, :],
                     op0=ALU.mult,
                     op1=ALU.add,
                 )
@@ -242,13 +249,15 @@ def tile_swintransformerblock_pb_t_kernel(tc, y, w1, b1, w2, b2, ln2_g, ln2_b, o
             if live(k + 1):
                 hidden = gelu(k + 1)
             if live(k + 2):
-                y_mx[k + 2] = quantise(work, collect_flipped(y_flipped[k + 2]), "y")
-                first_matmul(k + 2)
+                y_grouped = collect_flipped(y_flipped[k + 2])
             if live(k + 3):
                 if (k + 3) % GROUPS_IN_SLAB == 0 and live(k + 3 + GROUPS_IN_SLAB):
                     ahead = (k + 3) // GROUPS_IN_SLAB + 1
                     y_of_slab[ahead] = load_slab(ahead)
                 flip_tokens(k + 3)
+            if live(k + 2):
+                y_mx[k + 2] = quantise(work, y_grouped, "y")
+                first_matmul(k + 2)
             if live(k - 1):
                 scale_shift_store(k - 1)
             if live(k + 1):

@@ -16,7 +16,7 @@ PACK = 4
 CH = P * PACK
 WORDS = CH // 2
 IMAGES, WIN_ROWS, WIN_COLS, WS = 4, 4, 10, 8
-BLOCKS = 4
+BLOCKS = 2
 GROUP = BLOCKS * P
 GROUPS_IN_SLAB = WS // BLOCKS
 N_GROUPS = WIN_COLS * GROUPS_IN_SLAB
@@ -33,10 +33,11 @@ def tile_swintransformerblock_pb_t_kernel(tc, y, w1, b1, w2, b2, ln2_g, ln2_b, o
         const = ctx.enter_context(tc.tile_pool(name="const", bufs=1))
         slabs = ctx.enter_context(tc.tile_pool(name="slabs", bufs=3))
         work = ctx.enter_context(tc.tile_pool(name="work", bufs=2))
-        results = ctx.enter_context(tc.tile_pool(name="results", bufs=3))
-        psum_flip = ctx.enter_context(tc.psum_pool(name="psum_flip", bufs=2))
-        psum_hid = ctx.enter_context(tc.psum_pool(name="psum_hid", bufs=3))
-        psum_ffn = ctx.enter_context(tc.psum_pool(name="psum_ffn", bufs=2))
+        ahead = ctx.enter_context(tc.tile_pool(name="ahead", bufs=4))
+        results = ctx.enter_context(tc.tile_pool(name="results", bufs=5))
+        psum_flip = ctx.enter_context(tc.psum_pool(name="psum_flip", bufs=1))
+        psum_hid = ctx.enter_context(tc.psum_pool(name="psum_hid", bufs=4))
+        psum_ffn = ctx.enter_context(tc.psum_pool(name="psum_ffn", bufs=BLOCKS))
         psum_const = ctx.enter_context(tc.psum_pool(name="psum_const", bufs=1))
         ctx.enter_context(tc.manual_schedule())
 
@@ -46,44 +47,51 @@ def tile_swintransformerblock_pb_t_kernel(tc, y, w1, b1, w2, b2, ln2_g, ln2_b, o
                 nc.sync.dma_start(out=y_sb[r:P:WS, :], in_=y_slabs[ww, r])
             return y_sb
 
-        def flip_rows(words):
-            banks = []
-            for pair in range(BLOCKS // 2):
-                flipped = psum_flip.tile([P, 2, 2, P], F32)
-                for j in range(2):
-                    for u in range(2):
-                        first = ((2 * pair + j) * 2 + u) * P
-                        nc.tensor.transpose(flipped[:, j, u, :], words[:, first : first + P], ident[:])
-                banks.append(flipped)
-            return banks
+        def flip_rows(pool, words):
+            flipped = pool.tile([P, BLOCKS, 2, P], F32, tag="bank")
+            for j in range(BLOCKS):
+                for u in range(2):
+                    first = (j * 2 + u) * P
+                    nc.tensor.transpose(flipped[:, j, u, :], words[:, first : first + P], ident[:])
+            return flipped
 
-        def collect_flipped(banks):
+        def collect_flipped(flipped):
             grouped = work.tile([P, GROUP, PACK], BF16, align_bytes=64)
-            grouped_words = grouped[:].bitcast(F32)
-            for pair in range(BLOCKS // 2):
-                nc.scalar.copy(
-                    out=grouped_words[:, 2 * pair * P : 2 * (pair + 1) * P, :].rearrange("p (j r) u -> p j r u", j=2),
-                    in_=banks[pair][:].rearrange("p j u r -> p j r u"),
-                )
+            nc.scalar.copy(
+                out=grouped[:].bitcast(F32).rearrange("p (j r) u -> p j r u", j=BLOCKS),
+                in_=flipped[:].rearrange("p j u r -> p j r u"),
+            )
             return grouped
 
-        def quantise(pool, grouped, label):
-            codes = pool.tile([P, GROUP], U32, align_bytes=64, name=label + "_codes")
-            scales = pool.tile([P, GROUP], U8, align_bytes=64, name=label + "_scales")
-            nc.vector.quantize_mx(
-                out=codes[:].bitcast(FP8X4), scales=scales[:], in_=grouped[:].rearrange("p r t -> p (r t)")
-            )
+        def quantise(grouped, codes, scales):
+            nc.vector.quantize_mx(out=codes.bitcast(FP8X4), scales=scales, in_=grouped[:].rearrange("p r t -> p (r t)"))
+
+        def quantise_group(grouped, label):
+            codes = work.tile([P, GROUP], U32, align_bytes=64, name=label + "_codes")
+            scales = work.tile([P, GROUP], U8, align_bytes=64, name=label + "_scales")
+            quantise(grouped, codes[:], scales[:])
+            return codes, scales
+
+        def quantise_weight(w_sb, label):
+            codes = const.tile([P, CH], U32, align_bytes=64, name=label + "_codes")
+            scales = const.tile([P, CH], U8, align_bytes=64, name=label + "_scales")
+            words = w_sb[:].bitcast(F32)
+            span = BLOCKS * WORDS
+            banks = [flip_rows(psum_hid, words[:, h * span : (h + 1) * span]) for h in range(CH // GROUP)]
+            for h in range(CH // GROUP):
+                cols = slice(h * GROUP, (h + 1) * GROUP)
+                quantise(collect_flipped(banks[h]), codes[:, cols], scales[:, cols])
             return codes, scales
 
         ident = const.tile([P, P], F32)
         make_identity(nc, ident[:])
         minus_half = const.tile([P, BLOCKS], F32)
         nc.vector.memset(minus_half[:], -0.5)
+        ones = const.tile([P, P], BF16)
+        nc.vector.memset(ones[:], 1.0)
+        rows = const.tile([P, 3, CH], BF16)
+        nc.vector.memset(rows[:], 0.0)
 
-        b1_bf = const.tile([P, PACK], BF16)
-        nc.sync.dma_start(
-            out=b1_bf[:].rearrange("m (u e) -> m u e", u=2), in_=b1.rearrange("(u m e) -> m u e", u=2, e=2)
-        )
         w1_sb = const.tile([P, PACK * CH], BF16)
         nc.sync.dma_start(
             out=w1_sb[:].rearrange("m (u x) -> m u x", u=2), in_=w1.rearrange("(u m e) k -> m u (e k)", u=2, e=2)
@@ -93,34 +101,39 @@ def tile_swintransformerblock_pb_t_kernel(tc, y, w1, b1, w2, b2, ln2_g, ln2_b, o
         nc.sync.dma_start(
             out=w2_sb[:].rearrange("m (j f) -> m j f", j=PACK), in_=w2.rearrange("(j m) f -> m j f", m=P)
         )
-        b2_all = const.tile([P, CH], BF16)
-        nc.sync.dma_start(out=b2_all[:], in_=b2.partition_broadcast(P))
-        gain_all = const.tile([P, CH], BF16)
-        nc.sync.dma_start(out=gain_all[:], in_=ln2_g.partition_broadcast(P))
-        shift_all = const.tile([P, CH], BF16)
-        nc.sync.dma_start(out=shift_all[:], in_=ln2_b.partition_broadcast(P))
+        b1_bf = const.tile([P, PACK], BF16)
+        nc.gpsimd.dma_start(
+            out=b1_bf[:].rearrange("m (u e) -> m u e", u=2), in_=b1.rearrange("(u m e) -> m u e", u=2, e=2)
+        )
+        for i, vector in enumerate((b2, ln2_g, ln2_b)):
+            nc.gpsimd.dma_start(out=rows[0:1, i, :], in_=vector.rearrange("(o e) -> o e", o=1))
 
-        ident_bf = const.tile([P, P], BF16)
-        make_identity(nc, ident_bf[:])
-        gain_shift = psum_const.tile([P, 2, CH], BF16)
-        nc.tensor.matmul(out=gain_shift[:, 0, :], lhsT=ident_bf[:], rhs=gain_all[:], start=True, stop=True)
-        nc.tensor.matmul(out=gain_shift[:, 1, :], lhsT=ident_bf[:], rhs=shift_all[:], start=True, stop=True)
-
+        w1_codes, w1_scales = quantise_weight(w1_sb, "w1")
+        w2_codes, w2_scales = quantise_weight(w2_sb, "w2")
         b1_col = const.tile([P, PACK], F32)
         nc.vector.tensor_copy(out=b1_col[:], in_=b1_bf[:])
-        w1_codes, w1_scales = quantise(const, collect_flipped(flip_rows(w1_sb[:].bitcast(F32))), "w1")
-        w2_codes, w2_scales = quantise(const, collect_flipped(flip_rows(w2_sb[:].bitcast(F32))), "w2")
 
-        y_flipped, y_mx, hid_banks, h_mx, y_plus_b2, resid, neg_mean, rstd, normed = {}, {}, {}, {}, {}, {}, {}, {}, {}
+        b2_all = const.tile([P, CH], BF16)
+        gain_shift = psum_const.tile([P, 2, CH], BF16)
+
+        def spread_vectors():
+            b2_bank = psum_ffn.tile([P, CH], F32, tag="bank")
+            nc.tensor.matmul(out=b2_bank[:], lhsT=ones[:], rhs=rows[:, 0, :], start=True, stop=True)
+            nc.vector.tensor_copy(out=b2_all[:], in_=b2_bank[:])
+            nc.tensor.matmul(out=gain_shift[:, 0, :], lhsT=ones[:], rhs=rows[:, 1, :], start=True, stop=True)
+            nc.tensor.matmul(out=gain_shift[:, 1, :], lhsT=ones[:], rhs=rows[:, 2, :], start=True, stop=True)
+
+        y_flipped, y_mx, hid_banks, h_mx, ffn_banks = {}, {}, {}, {}, {}
+        y_plus_b2, resid, neg_mean, rstd, normed = {}, {}, {}, {}, {}
 
         def flip_tokens(g):
             words = y_of_slab[g // GROUPS_IN_SLAB][:].bitcast(F32)
             first = (g % GROUPS_IN_SLAB) * BLOCKS * WORDS
-            y_flipped[g] = flip_rows(words[:, first : first + BLOCKS * WORDS])
+            y_flipped[g] = flip_rows(psum_flip, words[:, first : first + BLOCKS * WORDS])
 
         def add_second_bias(g):
             y_sb = y_of_slab[g // GROUPS_IN_SLAB]
-            total = work.tile([P, BLOCKS, CH], F32, name="y_plus_b2")
+            total = ahead.tile([P, BLOCKS, CH], F32, name="y_plus_b2")
             for s in range(BLOCKS):
                 c = (g % GROUPS_IN_SLAB) * BLOCKS + s
                 nc.gpsimd.tensor_tensor(out=total[:, s, :], in0=y_sb[:, c * CH : (c + 1) * CH], in1=b2_all[:], op=ALU.add)
@@ -129,25 +142,30 @@ def tile_swintransformerblock_pb_t_kernel(tc, y, w1, b1, w2, b2, ln2_g, ln2_b, o
         def first_matmul(g):
             codes, scales = y_mx[g]
             hid_banks[g] = []
-            for t in range(PACK):
-                cols = slice(t * P, (t + 1) * P)
-                acc = psum_hid.tile([P, GROUP], F32)
-                nc.tensor.matmul_mx(
-                    out=acc[:],
-                    lhsT=w1_codes[:, cols].bitcast(FP8X4),
-                    lhsT_scale=w1_scales[:, cols],
-                    rhs=codes[:].bitcast(FP8X4),
-                    rhs_scale=scales[:],
-                    start=True,
-                    stop=True,
-                )
-                hid_banks[g].append(acc)
+            for u in range(2):
+                bank = psum_hid.tile([P, 2, GROUP], F32, tag="bank")
+                for e in range(2):
+                    cols = slice((2 * u + e) * P, (2 * u + e + 1) * P)
+                    nc.tensor.matmul_mx(
+                        out=bank[:, e, :],
+                        lhsT=w1_codes[:, cols].bitcast(FP8X4),
+                        lhsT_scale=w1_scales[:, cols],
+                        rhs=codes[:].bitcast(FP8X4),
+                        rhs_scale=scales[:],
+                        start=True,
+                        stop=True,
+                    )
+                hid_banks[g].append(bank)
 
         def gelu(g):
             hidden = work.tile([P, PACK, GROUP], BF16)
             for t in range(PACK):
                 nc.scalar.activation(
-                    out=hidden[:, t, :], in_=hid_banks[g][t][:], func=ACT.Gelu, bias=b1_col[:, t : t + 1], scale=1.0
+                    out=hidden[:, t, :],
+                    in_=hid_banks[g][t // 2][:, t % 2, :],
+                    func=ACT.Gelu,
+                    bias=b1_col[:, t : t + 1],
+                    scale=1.0,
                 )
             return hidden
 
@@ -161,13 +179,12 @@ def tile_swintransformerblock_pb_t_kernel(tc, y, w1, b1, w2, b2, ln2_g, ln2_b, o
 
         def second_matmul(g):
             codes, scales = h_mx[g]
-            total = work.tile([P, BLOCKS, CH], F32, name="resid")
-            row_sum = work.tile([P, BLOCKS], F32)
+            ffn_banks[g] = []
             for s in range(BLOCKS):
                 cols = slice(s * P, (s + 1) * P)
-                acc = psum_ffn.tile([P, CH], F32)
+                bank = psum_ffn.tile([P, CH], F32, tag="bank")
                 nc.tensor.matmul_mx(
-                    out=acc[:],
+                    out=bank[:],
                     lhsT=codes[:, cols].bitcast(FP8X4),
                     lhsT_scale=scales[:, cols],
                     rhs=w2_codes[:].bitcast(FP8X4),
@@ -175,9 +192,15 @@ def tile_swintransformerblock_pb_t_kernel(tc, y, w1, b1, w2, b2, ln2_g, ln2_b, o
                     start=True,
                     stop=True,
                 )
+                ffn_banks[g].append(bank)
+
+        def residual(g):
+            total = work.tile([P, BLOCKS, CH], F32, name="resid")
+            row_sum = work.tile([P, BLOCKS], F32)
+            for s in range(BLOCKS):
                 nc.vector.scalar_tensor_tensor(
                     out=total[:, s, :],
-                    in0=acc[:],
+                    in0=ffn_banks[g][s][:],
                     scalar=1.0,
                     in1=y_plus_b2[g][:, s, :],
                     op0=ALU.mult,
@@ -204,7 +227,7 @@ def tile_swintransformerblock_pb_t_kernel(tc, y, w1, b1, w2, b2, ln2_g, ln2_b, o
             nc.gpsimd.tensor_scalar(
                 out=var_eps[:], in0=square_sum[:], scalar1=1.0 / CH, scalar2=LN_EPS, op0=ALU.mult, op1=ALU.add
             )
-            inv_std = work.tile([P, BLOCKS], F32)
+            inv_std = ahead.tile([P, BLOCKS], F32)
             nc.gpsimd.tensor_tensor(out=inv_std[:], in0=var_eps[:], in1=minus_half[:], op=ALU.pow)
             rstd[g] = inv_std
 
@@ -241,27 +264,37 @@ def tile_swintransformerblock_pb_t_kernel(tc, y, w1, b1, w2, b2, ln2_g, ln2_b, o
         def live(g):
             return 0 <= g < N_GROUPS
 
-        for k in range(-3, N_GROUPS + 1):
-            if live(k + 1):
-                add_second_bias(k + 1)
-            if live(k):
-                second_matmul(k)
-            if live(k + 1):
-                hidden = gelu(k + 1)
-            if live(k + 2):
-                y_grouped = collect_flipped(y_flipped[k + 2])
+        def step(k):
             if live(k + 3):
-                if (k + 3) % GROUPS_IN_SLAB == 0 and live(k + 3 + GROUPS_IN_SLAB):
-                    ahead = (k + 3) // GROUPS_IN_SLAB + 1
-                    y_of_slab[ahead] = load_slab(ahead)
-                flip_tokens(k + 3)
-            if live(k + 2):
-                y_mx[k + 2] = quantise(work, y_grouped, "y")
-                first_matmul(k + 2)
-            if live(k - 1):
-                scale_shift_store(k - 1)
+                first_matmul(k + 3)
+            if live(k):
+                residual(k)
             if live(k + 1):
-                h_mx[k + 1] = quantise(work, regroup(hidden), "h")
+                second_matmul(k + 1)
+            if live(k + 2):
+                hidden = gelu(k + 2)
+            if live(k + 4):
+                y_grouped = collect_flipped(y_flipped[k + 4])
+            if live(k + 5):
+                if (k + 5) % GROUPS_IN_SLAB == 0 and live(k + 5 + GROUPS_IN_SLAB):
+                    following = (k + 5) // GROUPS_IN_SLAB + 1
+                    y_of_slab[following] = load_slab(following)
+                flip_tokens(k + 5)
+            if live(k + 4):
+                y_mx[k + 4] = quantise_group(y_grouped, "y")
+            if live(k - 2):
+                scale_shift_store(k - 2)
+            if live(k + 2):
+                h_mx[k + 2] = quantise_group(regroup(hidden), "h")
+                add_second_bias(k + 2)
             if live(k):
                 variance(k)
                 centre_and_gain(k)
+
+        FIRST_STEP = -5
+        VECTORS_STEP = -2
+        for k in range(FIRST_STEP, VECTORS_STEP):
+            step(k)
+        spread_vectors()
+        for k in range(VECTORS_STEP, N_GROUPS + 2):
+            step(k)

@@ -32,9 +32,9 @@ def tile_swintransformerblock_pb_t_kernel(tc, y, w1, b1, w2, b2, ln2_g, ln2_b, o
     with ExitStack() as ctx:
         const = ctx.enter_context(tc.tile_pool(name="const", bufs=1))
         slabs = ctx.enter_context(tc.tile_pool(name="slabs", bufs=3))
-        work = ctx.enter_context(tc.tile_pool(name="work", bufs=2))
+        work = ctx.enter_context(tc.tile_pool(name="work", bufs=3))
         ahead = ctx.enter_context(tc.tile_pool(name="ahead", bufs=4))
-        results = ctx.enter_context(tc.tile_pool(name="results", bufs=5))
+        results = ctx.enter_context(tc.tile_pool(name="results", bufs=6))
         psum_flip = ctx.enter_context(tc.psum_pool(name="psum_flip", bufs=1))
         psum_hid = ctx.enter_context(tc.psum_pool(name="psum_hid", bufs=4))
         psum_ffn = ctx.enter_context(tc.psum_pool(name="psum_ffn", bufs=BLOCKS))
@@ -123,7 +123,7 @@ def tile_swintransformerblock_pb_t_kernel(tc, y, w1, b1, w2, b2, ln2_g, ln2_b, o
             nc.tensor.matmul(out=gain_shift[:, 0, :], lhsT=ones[:], rhs=rows[:, 1, :], start=True, stop=True)
             nc.tensor.matmul(out=gain_shift[:, 1, :], lhsT=ones[:], rhs=rows[:, 2, :], start=True, stop=True)
 
-        y_flipped, y_mx, hid_banks, h_mx, ffn_banks = {}, {}, {}, {}, {}
+        y_flipped, y_grouped, y_mx, hid_banks, h_grouped, h_mx, ffn_banks = {}, {}, {}, {}, {}, {}, {}
         y_plus_b2, resid, neg_mean, rstd, normed = {}, {}, {}, {}, {}
 
         def flip_tokens(g):
@@ -195,7 +195,7 @@ def tile_swintransformerblock_pb_t_kernel(tc, y, w1, b1, w2, b2, ln2_g, ln2_b, o
                 ffn_banks[g].append(bank)
 
         def residual(g):
-            total = work.tile([P, BLOCKS, CH], F32, name="resid")
+            total = ahead.tile([P, BLOCKS, CH], F32, name="resid")
             row_sum = work.tile([P, BLOCKS], F32)
             for s in range(BLOCKS):
                 nc.vector.scalar_tensor_tensor(
@@ -207,7 +207,7 @@ def tile_swintransformerblock_pb_t_kernel(tc, y, w1, b1, w2, b2, ln2_g, ln2_b, o
                     op1=ALU.add,
                     accum_out=row_sum[:, s : s + 1],
                 )
-            minus_mean = work.tile([P, BLOCKS], F32)
+            minus_mean = ahead.tile([P, BLOCKS], F32)
             nc.vector.tensor_scalar_mul(out=minus_mean[:], in0=row_sum[:], scalar1=-1.0 / CH)
             resid[g], neg_mean[g] = total, minus_mean
 
@@ -265,36 +265,40 @@ def tile_swintransformerblock_pb_t_kernel(tc, y, w1, b1, w2, b2, ln2_g, ln2_b, o
             return 0 <= g < N_GROUPS
 
         def step(k):
-            if live(k + 3):
-                first_matmul(k + 3)
+            if live(k + 4):
+                first_matmul(k + 4)
             if live(k):
                 residual(k)
             if live(k + 1):
                 second_matmul(k + 1)
-            if live(k + 2):
-                hidden = gelu(k + 2)
-            if live(k + 4):
-                y_grouped = collect_flipped(y_flipped[k + 4])
+            if live(k + 3):
+                hidden = gelu(k + 3)
             if live(k + 5):
-                if (k + 5) % GROUPS_IN_SLAB == 0 and live(k + 5 + GROUPS_IN_SLAB):
-                    following = (k + 5) // GROUPS_IN_SLAB + 1
-                    y_of_slab[following] = load_slab(following)
-                flip_tokens(k + 5)
-            if live(k + 4):
-                y_mx[k + 4] = quantise_group(y_grouped, "y")
-            if live(k - 2):
-                scale_shift_store(k - 2)
+                y_mx[k + 5] = quantise_group(y_grouped[k + 5], "y")
             if live(k + 2):
-                h_mx[k + 2] = quantise_group(regroup(hidden), "h")
+                h_mx[k + 2] = quantise_group(h_grouped[k + 2], "h")
+            if live(k + 6):
+                y_grouped[k + 6] = collect_flipped(y_flipped[k + 6])
+            if live(k + 7):
+                if (k + 7) % GROUPS_IN_SLAB == 0 and live(k + 7 + GROUPS_IN_SLAB):
+                    following = (k + 7) // GROUPS_IN_SLAB + 1
+                    y_of_slab[following] = load_slab(following)
+                flip_tokens(k + 7)
+            if live(k - 3):
+                scale_shift_store(k - 3)
+            if live(k + 2):
                 add_second_bias(k + 2)
+            if live(k + 3):
+                h_grouped[k + 3] = regroup(hidden)
+            if live(k - 1):
+                variance(k - 1)
             if live(k):
-                variance(k)
                 centre_and_gain(k)
 
-        FIRST_STEP = -5
+        FIRST_STEP = -7
         VECTORS_STEP = -2
         for k in range(FIRST_STEP, VECTORS_STEP):
             step(k)
         spread_vectors()
-        for k in range(VECTORS_STEP, N_GROUPS + 2):
+        for k in range(VECTORS_STEP, N_GROUPS + 3):
             step(k)

@@ -34,6 +34,7 @@ def tile_swintransformerblock_pb_t_kernel(tc, y, w1, b1, w2, b2, ln2_g, ln2_b, o
         slabs = ctx.enter_context(tc.tile_pool(name="slabs", bufs=3))
         work = ctx.enter_context(tc.tile_pool(name="work", bufs=3))
         ahead = ctx.enter_context(tc.tile_pool(name="ahead", bufs=4))
+        sums = ctx.enter_context(tc.tile_pool(name="sums", bufs=2))
         results = ctx.enter_context(tc.tile_pool(name="results", bufs=6))
         psum_flip = ctx.enter_context(tc.psum_pool(name="psum_flip", bufs=1))
         psum_hid = ctx.enter_context(tc.psum_pool(name="psum_hid", bufs=4))
@@ -133,7 +134,7 @@ def tile_swintransformerblock_pb_t_kernel(tc, y, w1, b1, w2, b2, ln2_g, ln2_b, o
 
         def add_second_bias(g):
             y_sb = y_of_slab[g // GROUPS_IN_SLAB]
-            total = ahead.tile([P, BLOCKS, CH], F32, name="y_plus_b2")
+            total = sums.tile([P, BLOCKS, CH], F32, name="y_plus_b2")
             for s in range(BLOCKS):
                 c = (g % GROUPS_IN_SLAB) * BLOCKS + s
                 nc.gpsimd.tensor_tensor(out=total[:, s, :], in0=y_sb[:, c * CH : (c + 1) * CH], in1=b2_all[:], op=ALU.add)

@@ -56,22 +56,14 @@ def tile_swintransformerblock_pb_t_kernel(tc, y, w1, b1, w2, b2, ln2_g, ln2_b, o
                     nc.tensor.transpose(flipped[:, j, u, :], words[:, first : first + P], ident[:])
             return flipped
 
-        def collect_flipped(flipped):
-            grouped = work.tile([P, GROUP, PACK], BF16, align_bytes=64)
+        def collect_flipped(flipped, grouped):
             nc.scalar.copy(
-                out=grouped[:].bitcast(F32).rearrange("p (j r) u -> p j r u", j=BLOCKS),
+                out=grouped.rearrange("p r t -> p (r t)").bitcast(F32).rearrange("p (j r u) -> p j r u", j=BLOCKS, u=2),
                 in_=flipped[:].rearrange("p j u r -> p j r u"),
             )
-            return grouped
 
         def quantise(grouped, codes, scales):
-            nc.vector.quantize_mx(out=codes.bitcast(FP8X4), scales=scales, in_=grouped[:].rearrange("p r t -> p (r t)"))
-
-        def quantise_group(grouped, label):
-            codes = work.tile([P, GROUP], U32, align_bytes=64, name=label + "_codes")
-            scales = work.tile([P, GROUP], U8, align_bytes=64, name=label + "_scales")
-            quantise(grouped, codes[:], scales[:])
-            return codes, scales
+            nc.vector.quantize_mx(out=codes.bitcast(FP8X4), scales=scales, in_=grouped)
 
         def quantise_weight(w_sb, label):
             codes = const.tile([P, CH], U32, align_bytes=64, name=label + "_codes")
@@ -81,7 +73,9 @@ def tile_swintransformerblock_pb_t_kernel(tc, y, w1, b1, w2, b2, ln2_g, ln2_b, o
             banks = [flip_rows(psum_hid, words[:, h * span : (h + 1) * span]) for h in range(CH // GROUP)]
             for h in range(CH // GROUP):
                 cols = slice(h * GROUP, (h + 1) * GROUP)
-                quantise(collect_flipped(banks[h]), codes[:, cols], scales[:, cols])
+                grouped = work.tile([P, GROUP, PACK], BF16, align_bytes=64)
+                collect_flipped(banks[h], grouped[:])
+                quantise(grouped[:].rearrange("p r t -> p (r t)"), codes[:, cols], scales[:, cols])
             return codes, scales
 
         ident = const.tile([P, P], F32)
@@ -124,7 +118,10 @@ def tile_swintransformerblock_pb_t_kernel(tc, y, w1, b1, w2, b2, ln2_g, ln2_b, o
             nc.tensor.matmul(out=gain_shift[:, 0, :], lhsT=ones[:], rhs=rows[:, 1, :], start=True, stop=True)
             nc.tensor.matmul(out=gain_shift[:, 1, :], lhsT=ones[:], rhs=rows[:, 2, :], start=True, stop=True)
 
-        y_flipped, y_grouped, y_mx, hid_banks, h_grouped, h_mx, ffn_banks = {}, {}, {}, {}, {}, {}, {}
+        def live(g):
+            return 0 <= g < N_GROUPS
+
+        y_flipped, to_quantise, y_mx, hid_banks, h_mx, ffn_banks = {}, {}, {}, {}, {}, {}
         y_plus_b2, resid, neg_mean, rstd, normed = {}, {}, {}, {}, {}
 
         def flip_tokens(g):
@@ -140,6 +137,24 @@ def tile_swintransformerblock_pb_t_kernel(tc, y, w1, b1, w2, b2, ln2_g, ln2_b, o
                 nc.gpsimd.tensor_tensor(out=total[:, s, :], in0=y_sb[:, c * CH : (c + 1) * CH], in1=b2_all[:], op=ALU.add)
             y_plus_b2[g] = total
 
+        def pair_for(k):
+            if k not in to_quantise:
+                to_quantise[k] = ahead.tile([P, 2, GROUP, PACK], BF16, align_bytes=64, name="pair")
+            return to_quantise[k]
+
+        def quantise_pair(k):
+            codes = ahead.tile([P, 2, GROUP], U32, align_bytes=64, name="pair_codes")
+            scales = ahead.tile([P, 2, GROUP], U8, align_bytes=64, name="pair_scales")
+            has_y, has_h = live(k + 5), live(k + 2)
+            halves = slice(0 if has_y else 1, 2 if has_h else 1)
+            quantise(
+                pair_for(k)[:, halves].rearrange("p s r t -> p (s r t)"),
+                codes[:, halves].rearrange("p s r -> p (s r)"),
+                scales[:, halves].rearrange("p s r -> p (s r)"),
+            )
+            y_mx[k + 5] = codes[:, 0, :], scales[:, 0, :]
+            h_mx[k + 2] = codes[:, 1, :], scales[:, 1, :]
+
         def first_matmul(g):
             codes, scales = y_mx[g]
             hid_banks[g] = []
@@ -151,8 +166,8 @@ def tile_swintransformerblock_pb_t_kernel(tc, y, w1, b1, w2, b2, ln2_g, ln2_b, o
                         out=bank[:, e, :],
                         lhsT=w1_codes[:, cols].bitcast(FP8X4),
                         lhsT_scale=w1_scales[:, cols],
-                        rhs=codes[:].bitcast(FP8X4),
-                        rhs_scale=scales[:],
+                        rhs=codes.bitcast(FP8X4),
+                        rhs_scale=scales,
                         start=True,
                         stop=True,
                     )
@@ -170,13 +185,11 @@ def tile_swintransformerblock_pb_t_kernel(tc, y, w1, b1, w2, b2, ln2_g, ln2_b, o
                 )
             return hidden
 
-        def regroup(hidden):
-            grouped = work.tile([P, GROUP, PACK], BF16, align_bytes=64, name="h_grouped")
+        def regroup(hidden, grouped):
             nc.scalar.copy(
-                out=grouped[:].rearrange("p (c i) t -> p c t i", i=4),
+                out=grouped.rearrange("p (c i) t -> p c t i", i=4),
                 in_=hidden[:].rearrange("p t (c i) -> p c t i", i=4),
             )
-            return grouped
 
         def second_matmul(g):
             codes, scales = h_mx[g]
@@ -262,9 +275,6 @@ def tile_swintransformerblock_pb_t_kernel(tc, y, w1, b1, w2, b2, ln2_g, ln2_b, o
                 in_=scaled[:].rearrange("p s e -> p (s e)"),
             )
 
-        def live(g):
-            return 0 <= g < N_GROUPS
-
         def step(k):
             if live(k + 4):
                 first_matmul(k + 4)
@@ -274,12 +284,10 @@ def tile_swintransformerblock_pb_t_kernel(tc, y, w1, b1, w2, b2, ln2_g, ln2_b, o
                 second_matmul(k + 1)
             if live(k + 3):
                 hidden = gelu(k + 3)
-            if live(k + 5):
-                y_mx[k + 5] = quantise_group(y_grouped[k + 5], "y")
-            if live(k + 2):
-                h_mx[k + 2] = quantise_group(h_grouped[k + 2], "h")
+            if live(k + 5) or live(k + 2):
+                quantise_pair(k)
             if live(k + 6):
-                y_grouped[k + 6] = collect_flipped(y_flipped[k + 6])
+                collect_flipped(y_flipped[k + 6], pair_for(k + 1)[:, 0])
             if live(k + 7):
                 if (k + 7) % GROUPS_IN_SLAB == 0 and live(k + 7 + GROUPS_IN_SLAB):
                     following = (k + 7) // GROUPS_IN_SLAB + 1
@@ -290,7 +298,7 @@ def tile_swintransformerblock_pb_t_kernel(tc, y, w1, b1, w2, b2, ln2_g, ln2_b, o
             if live(k + 2):
                 add_second_bias(k + 2)
             if live(k + 3):
-                h_grouped[k + 3] = regroup(hidden)
+                regroup(hidden, pair_for(k + 1)[:, 1])
             if live(k - 1):
                 variance(k - 1)
             if live(k):

@@ -108,13 +108,14 @@ def tile_swintransformerblock_pb_t_kernel(tc, y, w1, b1, w2, b2, ln2_g, ln2_b, o
         b1_col = const.tile([P, PACK], F32)
         nc.vector.tensor_copy(out=b1_col[:], in_=b1_bf[:])
 
-        b2_all = const.tile([P, CH], BF16)
+        b2_all = const.tile([P, BLOCKS, CH], BF16)
         gain_shift = psum_const.tile([P, 2, CH], BF16)
 
         def spread_vectors():
             b2_bank = psum_ffn.tile([P, CH], F32, tag="bank")
             nc.tensor.matmul(out=b2_bank[:], lhsT=ones[:], rhs=rows[:, 0, :], start=True, stop=True)
-            nc.vector.tensor_copy(out=b2_all[:], in_=b2_bank[:])
+            for s in range(BLOCKS):
+                nc.vector.tensor_copy(out=b2_all[:, s, :], in_=b2_bank[:])
             nc.tensor.matmul(out=gain_shift[:, 0, :], lhsT=ones[:], rhs=rows[:, 1, :], start=True, stop=True)
             nc.tensor.matmul(out=gain_shift[:, 1, :], lhsT=ones[:], rhs=rows[:, 2, :], start=True, stop=True)
 
@@ -132,9 +133,13 @@ def tile_swintransformerblock_pb_t_kernel(tc, y, w1, b1, w2, b2, ln2_g, ln2_b, o
         def add_second_bias(g):
             y_sb = y_of_slab[g // GROUPS_IN_SLAB]
             total = sums.tile([P, BLOCKS, CH], F32, name="y_plus_b2")
-            for s in range(BLOCKS):
-                c = (g % GROUPS_IN_SLAB) * BLOCKS + s
-                nc.gpsimd.tensor_tensor(out=total[:, s, :], in0=y_sb[:, c * CH : (c + 1) * CH], in1=b2_all[:], op=ALU.add)
+            first = (g % GROUPS_IN_SLAB) * BLOCKS * CH
+            nc.gpsimd.tensor_tensor(
+                out=total[:].rearrange("p s e -> p (s e)"),
+                in0=y_sb[:, first : first + BLOCKS * CH],
+                in1=b2_all[:].rearrange("p s e -> p (s e)"),
+                op=ALU.add,
+            )
             y_plus_b2[g] = total
 
         def pair_for(k):
@@ -174,10 +179,10 @@ def tile_swintransformerblock_pb_t_kernel(tc, y, w1, b1, w2, b2, ln2_g, ln2_b, o
                 hid_banks[g].append(bank)
 
         def gelu(g):
-            hidden = work.tile([P, PACK, GROUP], BF16)
+            hidden = work.tile([P, 2, GROUP, 2], BF16)
             for t in range(PACK):
                 nc.scalar.activation(
-                    out=hidden[:, t, :],
+                    out=hidden[:, t // 2, :, t % 2],
                     in_=hid_banks[g][t // 2][:, t % 2, :],
                     func=ACT.Gelu,
                     bias=b1_col[:, t : t + 1],
@@ -187,8 +192,8 @@ def tile_swintransformerblock_pb_t_kernel(tc, y, w1, b1, w2, b2, ln2_g, ln2_b, o
 
         def regroup(hidden, grouped):
             nc.scalar.copy(
-                out=grouped.rearrange("p (c i) t -> p c t i", i=4),
-                in_=hidden[:].rearrange("p t (c i) -> p c t i", i=4),
+                out=grouped.rearrange("p r t -> p (r t)").bitcast(F32).rearrange("p (r u) -> p r u", u=2),
+                in_=hidden[:].rearrange("p u r e -> p (u r e)").bitcast(F32).rearrange("p (u r) -> p r u", u=2),
             )
 
         def second_matmul(g):

@@ -20,6 +20,7 @@ BLOCKS = 2
 GROUP = BLOCKS * P
 GROUPS_IN_SLAB = WS // BLOCKS
 N_GROUPS = WIN_COLS * GROUPS_IN_SLAB
+BY_VECTOR = 5
 LN_EPS = 1e-5
 FLOPS = 2 * 2 * IMAGES * WIN_ROWS * WIN_COLS * WS * WS * CH * CH
 
@@ -42,11 +43,17 @@ def tile_swintransformerblock_pb_t_kernel(tc, y, w1, b1, w2, b2, ln2_g, ln2_b, o
         psum_const = ctx.enter_context(tc.psum_pool(name="psum_const", bufs=1))
         ctx.enter_context(tc.manual_schedule())
 
-        def load_slab(ww):
+        def load_slab(ww, skip=0):
             y_sb = slabs.tile([P, WS * CH], BF16)
             for r in range(WS):
-                nc.sync.dma_start(out=y_sb[r:P:WS, :], in_=y_slabs[ww, r])
+                nc.sync.dma_start(out=y_sb[r:P:WS, skip:], in_=y_slabs[ww, r][:, skip:])
             return y_sb
+
+        def y_of_group(g):
+            if g == 0:
+                return y_first[:]
+            first = (g % GROUPS_IN_SLAB) * BLOCKS * CH
+            return y_of_slab[g // GROUPS_IN_SLAB][:, first : first + BLOCKS * CH]
 
         def flip_rows(pool, words):
             flipped = pool.tile([P, BLOCKS, 2, P], F32, tag="bank")
@@ -56,8 +63,8 @@ def tile_swintransformerblock_pb_t_kernel(tc, y, w1, b1, w2, b2, ln2_g, ln2_b, o
                     nc.tensor.transpose(flipped[:, j, u, :], words[:, first : first + P], ident[:])
             return flipped
 
-        def collect_flipped(flipped, grouped):
-            nc.scalar.copy(
+        def collect_flipped(flipped, grouped, copy):
+            copy(
                 out=grouped.rearrange("p r t -> p (r t)").bitcast(F32).rearrange("p (j r u) -> p j r u", j=BLOCKS, u=2),
                 in_=flipped[:].rearrange("p j u r -> p j r u"),
             )
@@ -65,21 +72,23 @@ def tile_swintransformerblock_pb_t_kernel(tc, y, w1, b1, w2, b2, ln2_g, ln2_b, o
         def quantise(grouped, codes, scales):
             nc.vector.quantize_mx(out=codes.bitcast(FP8X4), scales=scales, in_=grouped)
 
-        def quantise_weight(w_sb, label):
+        def quantise_weight(w_sb, label, copies):
             codes = const.tile([P, CH], U32, align_bytes=64, name=label + "_codes")
             scales = const.tile([P, CH], U8, align_bytes=64, name=label + "_scales")
             words = w_sb[:].bitcast(F32)
             span = BLOCKS * WORDS
             banks = [flip_rows(psum_hid, words[:, h * span : (h + 1) * span]) for h in range(CH // GROUP)]
+            grouped = work.tile([P, 2, GROUP, PACK], BF16, align_bytes=64, name=label + "_grouped")
             for h in range(CH // GROUP):
-                cols = slice(h * GROUP, (h + 1) * GROUP)
-                grouped = work.tile([P, GROUP, PACK], BF16, align_bytes=64)
-                collect_flipped(banks[h], grouped[:])
-                quantise(grouped[:].rearrange("p r t -> p (r t)"), codes[:, cols], scales[:, cols])
+                collect_flipped(banks[h], grouped[:, h], copies[h])
+            quantise(grouped[:].rearrange("p h r t -> p (h r t)"), codes[:], scales[:])
             return codes, scales
 
         ident = const.tile([P, P], F32)
         make_identity(nc, ident[:])
+        table = const.tile([P, 1], F32)
+        nc.vector.memset(table[:], 0.0)
+        nc.scalar.activation(out=table[:], in_=table[:], func=ACT.Gelu)
         minus_half = const.tile([P, BLOCKS], F32)
         nc.vector.memset(minus_half[:], -0.5)
         ones = const.tile([P, P], BF16)
@@ -91,56 +100,57 @@ def tile_swintransformerblock_pb_t_kernel(tc, y, w1, b1, w2, b2, ln2_g, ln2_b, o
         nc.sync.dma_start(
             out=w1_sb[:].rearrange("m (u x) -> m u x", u=2), in_=w1.rearrange("(u m e) k -> m u (e k)", u=2, e=2)
         )
-        y_of_slab = {0: load_slab(0)}
+        y_first = const.tile([P, BLOCKS * CH], BF16)
+        for r in range(WS):
+            queue = nc.gpsimd if r == WS - 1 else nc.sync
+            queue.dma_start(out=y_first[r:P:WS, :], in_=y_slabs[0, r][:, : BLOCKS * CH])
         w2_sb = const.tile([P, PACK * CH], BF16)
         nc.sync.dma_start(
             out=w2_sb[:].rearrange("m (j f) -> m j f", j=PACK), in_=w2.rearrange("(j m) f -> m j f", m=P)
         )
-        b1_bf = const.tile([P, PACK], BF16)
+        y_of_slab = {0: load_slab(0, skip=BLOCKS * CH)}
+        b1_col = const.tile([P, PACK], BF16)
         nc.gpsimd.dma_start(
-            out=b1_bf[:].rearrange("m (u e) -> m u e", u=2), in_=b1.rearrange("(u m e) -> m u e", u=2, e=2)
+            out=b1_col[:].rearrange("m (u e) -> m u e", u=2), in_=b1.rearrange("(u m e) -> m u e", u=2, e=2)
         )
         for i, vector in enumerate((b2, ln2_g, ln2_b)):
             nc.gpsimd.dma_start(out=rows[0:1, i, :], in_=vector.rearrange("(o e) -> o e", o=1))
 
-        w1_codes, w1_scales = quantise_weight(w1_sb, "w1")
-        w2_codes, w2_scales = quantise_weight(w2_sb, "w2")
-        b1_col = const.tile([P, PACK], F32)
-        nc.vector.tensor_copy(out=b1_col[:], in_=b1_bf[:])
-
-        b2_all = const.tile([P, BLOCKS, CH], BF16)
+        b2_all = const.tile([P, CH], BF16)
         gain_shift = psum_const.tile([P, 2, CH], BF16)
 
         def spread_vectors():
             b2_bank = psum_ffn.tile([P, CH], F32, tag="bank")
             nc.tensor.matmul(out=b2_bank[:], lhsT=ones[:], rhs=rows[:, 0, :], start=True, stop=True)
-            for s in range(BLOCKS):
-                nc.vector.tensor_copy(out=b2_all[:, s, :], in_=b2_bank[:])
+            nc.vector.tensor_copy(out=b2_all[:], in_=b2_bank[:])
             nc.tensor.matmul(out=gain_shift[:, 0, :], lhsT=ones[:], rhs=rows[:, 1, :], start=True, stop=True)
             nc.tensor.matmul(out=gain_shift[:, 1, :], lhsT=ones[:], rhs=rows[:, 2, :], start=True, stop=True)
 
         def live(g):
             return 0 <= g < N_GROUPS
 
-        y_flipped, to_quantise, y_mx, hid_banks, h_mx, ffn_banks = {}, {}, {}, {}, {}, {}
-        y_plus_b2, resid, neg_mean, rstd, normed = {}, {}, {}, {}, {}
+        y_flipped, to_quantise, y_mx, hid_banks, hidden_of, h_mx, ffn_banks = {}, {}, {}, {}, {}, {}, {}
+        y_plus_b2, resid, sums_of_rows, neg_mean, rstd, normed = {}, {}, {}, {}, {}, {}
 
         def flip_tokens(g):
-            words = y_of_slab[g // GROUPS_IN_SLAB][:].bitcast(F32)
-            first = (g % GROUPS_IN_SLAB) * BLOCKS * WORDS
-            y_flipped[g] = flip_rows(psum_flip, words[:, first : first + BLOCKS * WORDS])
+            if g % GROUPS_IN_SLAB == 0 and live(g + GROUPS_IN_SLAB):
+                following = g // GROUPS_IN_SLAB + 1
+                y_of_slab[following] = load_slab(following)
+            y_flipped[g] = flip_rows(psum_flip, y_of_group(g).bitcast(F32))
 
         def add_second_bias(g):
-            y_sb = y_of_slab[g // GROUPS_IN_SLAB]
             total = sums.tile([P, BLOCKS, CH], F32, name="y_plus_b2")
-            first = (g % GROUPS_IN_SLAB) * BLOCKS * CH
             nc.gpsimd.tensor_tensor(
-                out=total[:].rearrange("p s e -> p (s e)"),
-                in0=y_sb[:, first : first + BLOCKS * CH],
-                in1=b2_all[:].rearrange("p s e -> p (s e)"),
+                out=total[:],
+                in0=y_of_group(g).rearrange("p (s e) -> p s e", s=BLOCKS),
+                in1=b2_all[:].unsqueeze(1).to_broadcast([P, BLOCKS, CH]),
                 op=ALU.add,
             )
             y_plus_b2[g] = total
+
+        def collect_tokens(g):
+            copy = nc.vector.tensor_copy if 0 < g < BY_VECTOR else nc.scalar.copy
+            collect_flipped(y_flipped[g], pair_for(g - 4)[:, 0], copy)
 
         def pair_for(k):
             if k not in to_quantise:
@@ -150,15 +160,15 @@ def tile_swintransformerblock_pb_t_kernel(tc, y, w1, b1, w2, b2, ln2_g, ln2_b, o
         def quantise_pair(k):
             codes = ahead.tile([P, 2, GROUP], U32, align_bytes=64, name="pair_codes")
             scales = ahead.tile([P, 2, GROUP], U8, align_bytes=64, name="pair_scales")
-            has_y, has_h = live(k + 5), live(k + 2)
+            has_y, has_h = live(k + 4), live(k + 1)
             halves = slice(0 if has_y else 1, 2 if has_h else 1)
             quantise(
                 pair_for(k)[:, halves].rearrange("p s r t -> p (s r t)"),
                 codes[:, halves].rearrange("p s r -> p (s r)"),
                 scales[:, halves].rearrange("p s r -> p (s r)"),
             )
-            y_mx[k + 5] = codes[:, 0, :], scales[:, 0, :]
-            h_mx[k + 2] = codes[:, 1, :], scales[:, 1, :]
+            y_mx[k + 4] = codes[:, 0, :], scales[:, 0, :]
+            h_mx[k + 1] = codes[:, 1, :], scales[:, 1, :]
 
         def first_matmul(g):
             codes, scales = y_mx[g]
@@ -188,12 +198,13 @@ def tile_swintransformerblock_pb_t_kernel(tc, y, w1, b1, w2, b2, ln2_g, ln2_b, o
                     bias=b1_col[:, t : t + 1],
                     scale=1.0,
                 )
-            return hidden
+            hidden_of[g] = hidden
 
-        def regroup(hidden, grouped):
+        def regroup(g):
+            grouped = pair_for(g - 1)[:, 1]
             nc.scalar.copy(
                 out=grouped.rearrange("p r t -> p (r t)").bitcast(F32).rearrange("p (r u) -> p r u", u=2),
-                in_=hidden[:].rearrange("p u r e -> p (u r e)").bitcast(F32).rearrange("p (u r) -> p r u", u=2),
+                in_=hidden_of[g][:].rearrange("p u r e -> p (u r e)").bitcast(F32).rearrange("p (u r) -> p r u", u=2),
             )
 
         def second_matmul(g):
@@ -226,9 +237,12 @@ def tile_swintransformerblock_pb_t_kernel(tc, y, w1, b1, w2, b2, ln2_g, ln2_b, o
                     op1=ALU.add,
                     accum_out=row_sum[:, s : s + 1],
                 )
+            resid[g], sums_of_rows[g] = total, row_sum
+
+        def negate_mean(g):
             minus_mean = ahead.tile([P, BLOCKS], F32)
-            nc.vector.tensor_scalar_mul(out=minus_mean[:], in0=row_sum[:], scalar1=-1.0 / CH)
-            resid[g], neg_mean[g] = total, minus_mean
+            nc.scalar.mul(out=minus_mean[:], in_=sums_of_rows[g][:], mul=-1.0 / CH)
+            neg_mean[g] = minus_mean
 
         def variance(g):
             square_sum = work.tile([P, BLOCKS], F32)
@@ -280,39 +294,54 @@ def tile_swintransformerblock_pb_t_kernel(tc, y, w1, b1, w2, b2, ln2_g, ln2_b, o
                 in_=scaled[:].rearrange("p s e -> p (s e)"),
             )
 
-        def step(k):
-            if live(k + 4):
-                first_matmul(k + 4)
-            if live(k):
-                residual(k)
-            if live(k + 1):
-                second_matmul(k + 1)
-            if live(k + 3):
-                hidden = gelu(k + 3)
-            if live(k + 5) or live(k + 2):
-                quantise_pair(k)
-            if live(k + 6):
-                collect_flipped(y_flipped[k + 6], pair_for(k + 1)[:, 0])
-            if live(k + 7):
-                if (k + 7) % GROUPS_IN_SLAB == 0 and live(k + 7 + GROUPS_IN_SLAB):
-                    following = (k + 7) // GROUPS_IN_SLAB + 1
-                    y_of_slab[following] = load_slab(following)
-                flip_tokens(k + 7)
-            if live(k - 3):
-                scale_shift_store(k - 3)
-            if live(k + 2):
-                add_second_bias(k + 2)
-            if live(k + 3):
-                regroup(hidden, pair_for(k + 1)[:, 1])
-            if live(k - 1):
-                variance(k - 1)
-            if live(k):
-                centre_and_gain(k)
+        done = set()
 
-        FIRST_STEP = -7
-        VECTORS_STEP = -2
-        for k in range(FIRST_STEP, VECTORS_STEP):
-            step(k)
+        def run(stage, g):
+            if live(g) and (stage, g) not in done:
+                done.add((stage, g))
+                stage(g)
+
+        def run_quantise(k):
+            if (live(k + 4) or live(k + 1)) and (quantise_pair, k) not in done:
+                done.add((quantise_pair, k))
+                quantise_pair(k)
+
+        def step(k):
+            run(first_matmul, k + 3)
+            run(residual, k)
+            run(negate_mean, k - 1)
+            run(gelu, k + 2)
+            run_quantise(k)
+            run(second_matmul, k + 1)
+            run(collect_tokens, k + 5)
+            run(flip_tokens, k + 6)
+            run(scale_shift_store, k - 4)
+            run(add_second_bias, k + 2)
+            run(regroup, k + 2)
+            run(variance, k - 1)
+            run(centre_and_gain, k - 1)
+
+        w1_codes, w1_scales = quantise_weight(w1_sb, "w1", (nc.vector.tensor_copy, nc.scalar.copy))
+        run(flip_tokens, 0)
+        run(collect_tokens, 0)
+        run_quantise(-4)
+        run(first_matmul, 0)
+        run(gelu, 0)
+        run(flip_tokens, 1)
+        run(collect_tokens, 1)
         spread_vectors()
-        for k in range(VECTORS_STEP, N_GROUPS + 3):
+        run(flip_tokens, 2)
+        run_quantise(-3)
+        run(collect_tokens, 2)
+        w2_codes, w2_scales = quantise_weight(w2_sb, "w2", (nc.vector.tensor_copy, nc.vector.tensor_copy))
+        run(add_second_bias, 0)
+        run(first_matmul, 1)
+        run(flip_tokens, 3)
+        run(regroup, 0)
+        run_quantise(-2)
+        run(collect_tokens, 3)
+        run_quantise(-1)
+        run(second_matmul, 0)
+        run(gelu, 1)
+        for k in range(-2, N_GROUPS + 4):
             step(k)

@@ -20,7 +20,7 @@ BLOCKS = 2
 GROUP = BLOCKS * P
 GROUPS_IN_SLAB = WS // BLOCKS
 N_GROUPS = WIN_COLS * GROUPS_IN_SLAB
-BY_VECTOR = 5
+BY_VECTOR = 3
 LN_EPS = 1e-5
 FLOPS = 2 * 2 * IMAGES * WIN_ROWS * WIN_COLS * WS * WS * CH * CH
 
@@ -72,15 +72,18 @@ def tile_swintransformerblock_pb_t_kernel(tc, y, w1, b1, w2, b2, ln2_g, ln2_b, o
         def quantise(grouped, codes, scales):
             nc.vector.quantize_mx(out=codes.bitcast(FP8X4), scales=scales, in_=grouped)
 
-        def quantise_weight(w_sb, label, copies):
-            codes = const.tile([P, CH], U32, align_bytes=64, name=label + "_codes")
-            scales = const.tile([P, CH], U8, align_bytes=64, name=label + "_scales")
+        def group_weight(w_sb, label, pool, copies):
             words = w_sb[:].bitcast(F32)
             span = BLOCKS * WORDS
-            banks = [flip_rows(psum_hid, words[:, h * span : (h + 1) * span]) for h in range(CH // GROUP)]
+            banks = [flip_rows(pool, words[:, h * span : (h + 1) * span]) for h in range(CH // GROUP)]
             grouped = work.tile([P, 2, GROUP, PACK], BF16, align_bytes=64, name=label + "_grouped")
             for h in range(CH // GROUP):
                 collect_flipped(banks[h], grouped[:, h], copies[h])
+            return grouped
+
+        def quantise_weight(grouped, label):
+            codes = const.tile([P, CH], U32, align_bytes=64, name=label + "_codes")
+            scales = const.tile([P, CH], U8, align_bytes=64, name=label + "_scales")
             quantise(grouped[:].rearrange("p h r t -> p (h r t)"), codes[:], scales[:])
             return codes, scales
 
@@ -104,14 +107,14 @@ def tile_swintransformerblock_pb_t_kernel(tc, y, w1, b1, w2, b2, ln2_g, ln2_b, o
         for r in range(WS):
             queue = nc.gpsimd if r == WS - 1 else nc.sync
             queue.dma_start(out=y_first[r:P:WS, :], in_=y_slabs[0, r][:, : BLOCKS * CH])
-        w2_sb = const.tile([P, PACK * CH], BF16)
-        nc.sync.dma_start(
-            out=w2_sb[:].rearrange("m (j f) -> m j f", j=PACK), in_=w2.rearrange("(j m) f -> m j f", m=P)
-        )
         y_of_slab = {0: load_slab(0, skip=BLOCKS * CH)}
         b1_col = const.tile([P, PACK], BF16)
         nc.gpsimd.dma_start(
             out=b1_col[:].rearrange("m (u e) -> m u e", u=2), in_=b1.rearrange("(u m e) -> m u e", u=2, e=2)
+        )
+        w2_sb = const.tile([P, PACK * CH], BF16)
+        nc.gpsimd.dma_start(
+            out=w2_sb[:].rearrange("m (j f) -> m j f", j=PACK), in_=w2.rearrange("(j m) f -> m j f", m=P)
         )
         for i, vector in enumerate((b2, ln2_g, ln2_b)):
             nc.gpsimd.dma_start(out=rows[0:1, i, :], in_=vector.rearrange("(o e) -> o e", o=1))
@@ -119,17 +122,13 @@ def tile_swintransformerblock_pb_t_kernel(tc, y, w1, b1, w2, b2, ln2_g, ln2_b, o
         b2_all = const.tile([P, CH], BF16)
         gain_shift = psum_const.tile([P, 2, CH], BF16)
 
-        def spread_vectors():
-            b2_bank = psum_ffn.tile([P, CH], F32, tag="bank")
-            nc.tensor.matmul(out=b2_bank[:], lhsT=ones[:], rhs=rows[:, 0, :], start=True, stop=True)
-            nc.vector.tensor_copy(out=b2_all[:], in_=b2_bank[:])
-            nc.tensor.matmul(out=gain_shift[:, 0, :], lhsT=ones[:], rhs=rows[:, 1, :], start=True, stop=True)
-            nc.tensor.matmul(out=gain_shift[:, 1, :], lhsT=ones[:], rhs=rows[:, 2, :], start=True, stop=True)
+        def spread_vector(i, bank):
+            nc.tensor.matmul(out=bank, lhsT=ones[:], rhs=rows[:, i, :], start=True, stop=True)
 
         def live(g):
             return 0 <= g < N_GROUPS
 
-        y_flipped, to_quantise, y_mx, hid_banks, hidden_of, h_mx, ffn_banks = {}, {}, {}, {}, {}, {}, {}
+        y_flipped, to_quantise, pair_codes, y_mx, hid_banks, hidden_of, h_mx, ffn_banks = {}, {}, {}, {}, {}, {}, {}, {}
         y_plus_b2, resid, sums_of_rows, neg_mean, rstd, normed = {}, {}, {}, {}, {}, {}
 
         def flip_tokens(g):
@@ -157,18 +156,28 @@ def tile_swintransformerblock_pb_t_kernel(tc, y, w1, b1, w2, b2, ln2_g, ln2_b, o
                 to_quantise[k] = ahead.tile([P, 2, GROUP, PACK], BF16, align_bytes=64, name="pair")
             return to_quantise[k]
 
-        def quantise_pair(k):
-            codes = ahead.tile([P, 2, GROUP], U32, align_bytes=64, name="pair_codes")
-            scales = ahead.tile([P, 2, GROUP], U8, align_bytes=64, name="pair_scales")
-            has_y, has_h = live(k + 4), live(k + 1)
-            halves = slice(0 if has_y else 1, 2 if has_h else 1)
+        def codes_for(k):
+            if k not in pair_codes:
+                codes = ahead.tile([P, 2, GROUP], U32, align_bytes=64, name="pair_codes")
+                scales = ahead.tile([P, 2, GROUP], U8, align_bytes=64, name="pair_scales")
+                pair_codes[k] = codes, scales
+                y_mx[k + 4] = codes[:, 0, :], scales[:, 0, :]
+                h_mx[k + 1] = codes[:, 1, :], scales[:, 1, :]
+            return pair_codes[k]
+
+        def quantise_halves(k, first, last):
+            codes, scales = codes_for(k)
             quantise(
-                pair_for(k)[:, halves].rearrange("p s r t -> p (s r t)"),
-                codes[:, halves].rearrange("p s r -> p (s r)"),
-                scales[:, halves].rearrange("p s r -> p (s r)"),
+                pair_for(k)[:, first : last + 1].rearrange("p s r t -> p (s r t)"),
+                codes[:, first : last + 1].rearrange("p s r -> p (s r)"),
+                scales[:, first : last + 1].rearrange("p s r -> p (s r)"),
             )
-            y_mx[k + 4] = codes[:, 0, :], scales[:, 0, :]
-            h_mx[k + 1] = codes[:, 1, :], scales[:, 1, :]
+
+        def quantise_y(g):
+            quantise_halves(g - 4, 0, 0)
+
+        def quantise_hidden(g):
+            quantise_halves(g - 1, 1, 1)
 
         def first_matmul(g):
             codes, scales = y_mx[g]
@@ -301,47 +310,70 @@ def tile_swintransformerblock_pb_t_kernel(tc, y, w1, b1, w2, b2, ln2_g, ln2_b, o
                 done.add((stage, g))
                 stage(g)
 
-        def run_quantise(k):
-            if (live(k + 4) or live(k + 1)) and (quantise_pair, k) not in done:
-                done.add((quantise_pair, k))
-                quantise_pair(k)
+        def quantise_pair(k):
+            y_due = live(k + 4) and (quantise_y, k + 4) not in done
+            h_due = live(k + 1) and (quantise_hidden, k + 1) not in done
+            if y_due and h_due:
+                done.add((quantise_y, k + 4))
+                done.add((quantise_hidden, k + 1))
+                quantise_halves(k, 0, 1)
+            run(quantise_y, k + 4)
+            run(quantise_hidden, k + 1)
 
         def step(k):
             run(first_matmul, k + 3)
             run(residual, k)
             run(negate_mean, k - 1)
             run(gelu, k + 2)
-            run_quantise(k)
+            quantise_pair(k)
             run(second_matmul, k + 1)
             run(collect_tokens, k + 5)
             run(flip_tokens, k + 6)
-            run(scale_shift_store, k - 4)
+            run(scale_shift_store, k - 3)
             run(add_second_bias, k + 2)
             run(regroup, k + 2)
             run(variance, k - 1)
             run(centre_and_gain, k - 1)
 
-        w1_codes, w1_scales = quantise_weight(w1_sb, "w1", (nc.vector.tensor_copy, nc.scalar.copy))
+        w1_grouped = group_weight(w1_sb, "w1", psum_hid, (nc.vector.tensor_copy, nc.scalar.copy))
+        w1_codes, w1_scales = quantise_weight(w1_grouped, "w1")
         run(flip_tokens, 0)
         run(collect_tokens, 0)
-        run_quantise(-4)
+        run(quantise_y, 0)
         run(first_matmul, 0)
         run(gelu, 0)
+        w2_grouped = group_weight(w2_sb, "w2", psum_ffn, (nc.vector.tensor_copy, nc.vector.tensor_copy))
         run(flip_tokens, 1)
         run(collect_tokens, 1)
-        spread_vectors()
-        run(flip_tokens, 2)
-        run_quantise(-3)
-        run(collect_tokens, 2)
-        w2_codes, w2_scales = quantise_weight(w2_sb, "w2", (nc.vector.tensor_copy, nc.vector.tensor_copy))
+        b2_bank = psum_ffn.tile([P, CH], F32, tag="bank")
+        spread_vector(0, b2_bank[:])
+        nc.vector.tensor_copy(out=b2_all[:], in_=b2_bank[:])
         run(add_second_bias, 0)
+        run(quantise_y, 1)
+        w2_codes, w2_scales = quantise_weight(w2_grouped, "w2")
         run(first_matmul, 1)
-        run(flip_tokens, 3)
         run(regroup, 0)
-        run_quantise(-2)
-        run(collect_tokens, 3)
-        run_quantise(-1)
-        run(second_matmul, 0)
         run(gelu, 1)
-        for k in range(-2, N_GROUPS + 4):
+        run(flip_tokens, 2)
+        run(quantise_hidden, 0)
+        run(second_matmul, 0)
+        spread_vector(1, gain_shift[:, 0, :])
+        spread_vector(2, gain_shift[:, 1, :])
+        run(collect_tokens, 2)
+        run(quantise_y, 2)
+        run(first_matmul, 2)
+        run(flip_tokens, 3)
+        run(residual, 0)
+        run(regroup, 1)
+        run(collect_tokens, 3)
+        run(quantise_hidden, 1)
+        run(second_matmul, 1)
+        run(add_second_bias, 1)
+        run(gelu, 2)
+        run(quantise_y, 3)
+        run(flip_tokens, 4)
+        run(collect_tokens, 4)
+        run(residual, 1)
+        run(flip_tokens, 5)
+        for k in range(N_GROUPS + 3):
             step(k)

@@ -20,7 +20,7 @@ BLOCKS = 2
 GROUP = BLOCKS * P
 GROUPS_IN_SLAB = WS // BLOCKS
 N_GROUPS = WIN_COLS * GROUPS_IN_SLAB
-BY_VECTOR = 3
+BY_VECTOR = 2
 LN_EPS = 1e-5
 FLOPS = 2 * 2 * IMAGES * WIN_ROWS * WIN_COLS * WS * WS * CH * CH
 
@@ -342,27 +342,27 @@ def tile_swintransformerblock_pb_t_kernel(tc, y, w1, b1, w2, b2, ln2_g, ln2_b, o
         run(quantise_y, 0)
         run(first_matmul, 0)
         run(gelu, 0)
-        w2_grouped = group_weight(w2_sb, "w2", psum_ffn, (nc.vector.tensor_copy, nc.vector.tensor_copy))
         run(flip_tokens, 1)
         run(collect_tokens, 1)
+        run(quantise_y, 1)
+        w2_grouped = group_weight(w2_sb, "w2", psum_ffn, (nc.vector.tensor_copy, nc.vector.tensor_copy))
+        run(first_matmul, 1)
         b2_bank = psum_ffn.tile([P, CH], F32, tag="bank")
         spread_vector(0, b2_bank[:])
         nc.vector.tensor_copy(out=b2_all[:], in_=b2_bank[:])
         run(add_second_bias, 0)
-        run(quantise_y, 1)
         w2_codes, w2_scales = quantise_weight(w2_grouped, "w2")
-        run(first_matmul, 1)
         run(regroup, 0)
-        run(gelu, 1)
         run(flip_tokens, 2)
+        run(collect_tokens, 2)
+        run(gelu, 1)
+        run(flip_tokens, 3)
         run(quantise_hidden, 0)
         run(second_matmul, 0)
-        spread_vector(1, gain_shift[:, 0, :])
-        spread_vector(2, gain_shift[:, 1, :])
-        run(collect_tokens, 2)
         run(quantise_y, 2)
         run(first_matmul, 2)
-        run(flip_tokens, 3)
+        spread_vector(1, gain_shift[:, 0, :])
+        spread_vector(2, gain_shift[:, 1, :])
         run(residual, 0)
         run(regroup, 1)
         run(collect_tokens, 3)

@@ -239,9 +239,9 @@ def tile_swintransformerblock_pb_t_kernel(tc, y, w1, b1, w2, b2, ln2_g, ln2_b, o
             for s in range(BLOCKS):
                 nc.vector.scalar_tensor_tensor(
                     out=total[:, s, :],
-                    in0=ffn_banks[g][s][:],
+                    in0=y_plus_b2[g][:, s, :],
                     scalar=1.0,
-                    in1=y_plus_b2[g][:, s, :],
+                    in1=ffn_banks[g][s][:],
                     op0=ALU.mult,
                     op1=ALU.add,
                     accum_out=row_sum[:, s : s + 1],

from contextlib import ExitStack

import concourse.mybir as mybir
from concourse.masks import make_identity

F32 = mybir.dt.float32
BF16 = mybir.dt.bfloat16
U32 = mybir.dt.uint32
U8 = mybir.dt.uint8
FP8X4 = mybir.dt.float8_e4m3fn_x4
ACT = mybir.ActivationFunctionType
ALU = mybir.AluOpType

P = 128
PACK = 4
CH = P * PACK
WORDS = CH // 2
IMAGES, WIN_ROWS, WIN_COLS, WS = 4, 4, 10, 8
BLOCKS = 2
GROUP = BLOCKS * P
GROUPS_IN_SLAB = WS // BLOCKS
N_GROUPS = WIN_COLS * GROUPS_IN_SLAB
BY_VECTOR = 2
LN_EPS = 1e-5
FLOPS = 2 * 2 * IMAGES * WIN_ROWS * WIN_COLS * WS * WS * CH * CH


def tile_swintransformerblock_pb_t_kernel(tc, y, w1, b1, w2, b2, ln2_g, ln2_b, out):
    nc = tc.nc
    y_slabs = y.rearrange("(iw ww) (r c) e -> ww r iw (c e)", ww=WIN_COLS, c=WS)
    out_slabs = out.rearrange("i (wr r ww c) e -> ww (i wr r) (c e)", wr=WIN_ROWS, r=WS, ww=WIN_COLS, c=WS)

    with ExitStack() as ctx:
        const = ctx.enter_context(tc.tile_pool(name="const", bufs=1))
        slabs = ctx.enter_context(tc.tile_pool(name="slabs", bufs=3))
        work = ctx.enter_context(tc.tile_pool(name="work", bufs=3))
        ahead = ctx.enter_context(tc.tile_pool(name="ahead", bufs=4))
        sums = ctx.enter_context(tc.tile_pool(name="sums", bufs=2))
        results = ctx.enter_context(tc.tile_pool(name="results", bufs=6))
        psum_flip = ctx.enter_context(tc.psum_pool(name="psum_flip", bufs=1))
        psum_hid = ctx.enter_context(tc.psum_pool(name="psum_hid", bufs=4))
        psum_ffn = ctx.enter_context(tc.psum_pool(name="psum_ffn", bufs=BLOCKS))
        psum_const = ctx.enter_context(tc.psum_pool(name="psum_const", bufs=1))
        ctx.enter_context(tc.manual_schedule())

        def load_slab(ww, skip=0):
            y_sb = slabs.tile([P, WS * CH], BF16)
            for r in range(WS):
                nc.sync.dma_start(out=y_sb[r:P:WS, skip:], in_=y_slabs[ww, r][:, skip:])
            return y_sb

        def y_of_group(g):
            if g == 0:
                return y_first[:]
            first = (g % GROUPS_IN_SLAB) * BLOCKS * CH
            return y_of_slab[g // GROUPS_IN_SLAB][:, first : first + BLOCKS * CH]

        def flip_rows(pool, words):
            flipped = pool.tile([P, BLOCKS, 2, P], F32, tag="bank")
            for j in range(BLOCKS):
                for u in range(2):
                    first = (j * 2 + u) * P
                    nc.tensor.transpose(flipped[:, j, u, :], words[:, first : first + P], ident[:])
            return flipped

        def collect_flipped(flipped, grouped, copy):
            copy(
                out=grouped.rearrange("p r t -> p (r t)").bitcast(F32).rearrange("p (j r u) -> p j r u", j=BLOCKS, u=2),
                in_=flipped[:].rearrange("p j u r -> p j r u"),
            )

        def quantise(grouped, codes, scales):
            nc.vector.quantize_mx(out=codes.bitcast(FP8X4), scales=scales, in_=grouped)

        def group_weight(w_sb, label, pool, copies):
            words = w_sb[:].bitcast(F32)
            span = BLOCKS * WORDS
            banks = [flip_rows(pool, words[:, h * span : (h + 1) * span]) for h in range(CH // GROUP)]
            grouped = work.tile([P, 2, GROUP, PACK], BF16, align_bytes=64, name=label + "_grouped")
            for h in range(CH // GROUP):
                collect_flipped(banks[h], grouped[:, h], copies[h])
            return grouped

        def quantise_weight(grouped, label):
            codes = const.tile([P, CH], U32, align_bytes=64, name=label + "_codes")
            scales = const.tile([P, CH], U8, align_bytes=64, name=label + "_scales")
            quantise(grouped[:].rearrange("p h r t -> p (h r t)"), codes[:], scales[:])
            return codes, scales

        ident = const.tile([P, P], F32)
        make_identity(nc, ident[:])
        table = const.tile([P, 1], F32)
        nc.vector.memset(table[:], 0.0)
        nc.scalar.activation(out=table[:], in_=table[:], func=ACT.Gelu)
        minus_half = const.tile([P, BLOCKS], F32)
        nc.vector.memset(minus_half[:], -0.5)
        ones = const.tile([P, P], BF16)
        nc.vector.memset(ones[:], 1.0)
        rows = const.tile([P, 3, CH], BF16)
        nc.vector.memset(rows[:], 0.0)

        w1_sb = const.tile([P, PACK * CH], BF16)
        nc.sync.dma_start(
            out=w1_sb[:].rearrange("m (u x) -> m u x", u=2), in_=w1.rearrange("(u m e) k -> m u (e k)", u=2, e=2)
        )
        y_first = const.tile([P, BLOCKS * CH], BF16)
        for r in range(WS):
            queue = nc.gpsimd if r == WS - 1 else nc.sync
            queue.dma_start(out=y_first[r:P:WS, :], in_=y_slabs[0, r][:, : BLOCKS * CH])
        y_of_slab = {0: load_slab(0, skip=BLOCKS * CH)}
        b1_col = const.tile([P, PACK], BF16)
        nc.gpsimd.dma_start(
            out=b1_col[:].rearrange("m (u e) -> m u e", u=2), in_=b1.rearrange("(u m e) -> m u e", u=2, e=2)
        )
        w2_sb = const.tile([P, PACK * CH], BF16)
        nc.gpsimd.dma_start(
            out=w2_sb[:].rearrange("m (j f) -> m j f", j=PACK), in_=w2.rearrange("(j m) f -> m j f", m=P)
        )
        for i, vector in enumerate((b2, ln2_g, ln2_b)):
            nc.gpsimd.dma_start(out=rows[0:1, i, :], in_=vector.rearrange("(o e) -> o e", o=1))

        b2_all = const.tile([P, CH], BF16)
        gain_shift = psum_const.tile([P, 2, CH], BF16)

        def spread_vector(i, bank):
            nc.tensor.matmul(out=bank, lhsT=ones[:], rhs=rows[:, i, :], start=True, stop=True)

        def live(g):
            return 0 <= g < N_GROUPS

        y_flipped, to_quantise, pair_codes, y_mx, hid_banks, hidden_of, h_mx, ffn_banks = {}, {}, {}, {}, {}, {}, {}, {}
        y_plus_b2, resid, sums_of_rows, neg_mean, rstd, normed = {}, {}, {}, {}, {}, {}

        def flip_tokens(g):
            if g % GROUPS_IN_SLAB == 0 and live(g + GROUPS_IN_SLAB):
                following = g // GROUPS_IN_SLAB + 1
                y_of_slab[following] = load_slab(following)
            y_flipped[g] = flip_rows(psum_flip, y_of_group(g).bitcast(F32))

        def add_second_bias(g):
            total = sums.tile([P, BLOCKS, CH], F32, name="y_plus_b2")
            nc.gpsimd.tensor_tensor(
                out=total[:],
                in0=y_of_group(g).rearrange("p (s e) -> p s e", s=BLOCKS),
                in1=b2_all[:].unsqueeze(1).to_broadcast([P, BLOCKS, CH]),
                op=ALU.add,
            )
            y_plus_b2[g] = total

        def collect_tokens(g):
            copy = nc.vector.tensor_copy if 0 < g < BY_VECTOR else nc.scalar.copy
            collect_flipped(y_flipped[g], pair_for(g - 4)[:, 0], copy)

        def pair_for(k):
            if k not in to_quantise:
                to_quantise[k] = ahead.tile([P, 2, GROUP, PACK], BF16, align_bytes=64, name="pair")
            return to_quantise[k]

        def codes_for(k):
            if k not in pair_codes:
                codes = ahead.tile([P, 2, GROUP], U32, align_bytes=64, name="pair_codes")
                scales = ahead.tile([P, 2, GROUP], U8, align_bytes=64, name="pair_scales")
                pair_codes[k] = codes, scales
                y_mx[k + 4] = codes[:, 0, :], scales[:, 0, :]
                h_mx[k + 1] = codes[:, 1, :], scales[:, 1, :]
            return pair_codes[k]

        def quantise_halves(k, first, last):
            codes, scales = codes_for(k)
            quantise(
                pair_for(k)[:, first : last + 1].rearrange("p s r t -> p (s r t)"),
                codes[:, first : last + 1].rearrange("p s r -> p (s r)"),
                scales[:, first : last + 1].rearrange("p s r -> p (s r)"),
            )

        def quantise_y(g):
            quantise_halves(g - 4, 0, 0)

        def quantise_hidden(g):
            quantise_halves(g - 1, 1, 1)

        def first_matmul(g):
            codes, scales = y_mx[g]
            hid_banks[g] = []
            for u in range(2):
                bank = psum_hid.tile([P, 2, GROUP], F32, tag="bank")
                for e in range(2):
                    cols = slice((2 * u + e) * P, (2 * u + e + 1) * P)
                    nc.tensor.matmul_mx(
                        out=bank[:, e, :],
                        lhsT=w1_codes[:, cols].bitcast(FP8X4),
                        lhsT_scale=w1_scales[:, cols],
                        rhs=codes.bitcast(FP8X4),
                        rhs_scale=scales,
                        start=True,
                        stop=True,
                    )
                hid_banks[g].append(bank)

        def gelu(g):
            hidden = work.tile([P, 2, GROUP, 2], BF16)
            for t in range(PACK):
                nc.scalar.activation(
                    out=hidden[:, t // 2, :, t % 2],
                    in_=hid_banks[g][t // 2][:, t % 2, :],
                    func=ACT.Gelu,
                    bias=b1_col[:, t : t + 1],
                    scale=1.0,
                )
            hidden_of[g] = hidden

        def regroup(g):
            grouped = pair_for(g - 1)[:, 1]
            nc.scalar.copy(
                out=grouped.rearrange("p r t -> p (r t)").bitcast(F32).rearrange("p (r u) -> p r u", u=2),
                in_=hidden_of[g][:].rearrange("p u r e -> p (u r e)").bitcast(F32).rearrange("p (u r) -> p r u", u=2),
            )

        def second_matmul(g):
            codes, scales = h_mx[g]
            ffn_banks[g] = []
            for s in range(BLOCKS):
                cols = slice(s * P, (s + 1) * P)
                bank = psum_ffn.tile([P, CH], F32, tag="bank")
                nc.tensor.matmul_mx(
                    out=bank[:],
                    lhsT=codes[:, cols].bitcast(FP8X4),
                    lhsT_scale=scales[:, cols],
                    rhs=w2_codes[:].bitcast(FP8X4),
                    rhs_scale=w2_scales[:],
                    start=True,
                    stop=True,
                )
                ffn_banks[g].append(bank)

        def residual(g):
            total = ahead.tile([P, BLOCKS, CH], F32, name="resid")
            row_sum = work.tile([P, BLOCKS], F32)
            for s in range(BLOCKS):
                nc.vector.scalar_tensor_tensor(
                    out=total[:, s, :],
                    in0=y_plus_b2[g][:, s, :],
                    scalar=1.0,
                    in1=ffn_banks[g][s][:],
                    op0=ALU.mult,
                    op1=ALU.add,
                    accum_out=row_sum[:, s : s + 1],
                )
            resid[g], sums_of_rows[g] = total, row_sum

        def negate_mean(g):
            minus_mean = ahead.tile([P, BLOCKS], F32)
            nc.scalar.mul(out=minus_mean[:], in_=sums_of_rows[g][:], mul=-1.0 / CH)
            neg_mean[g] = minus_mean

        def variance(g):
            square_sum = work.tile([P, BLOCKS], F32)
            for s in range(BLOCKS):
                squares = work.tile([P, CH], F32)
                nc.scalar.activation(
                    out=squares[:],
                    in_=resid[g][:, s, :],
                    func=ACT.Square,
                    bias=neg_mean[g][:, s : s + 1],
                    scale=1.0,
                    accum_out=square_sum[:, s : s + 1],
                )
            var_eps = work.tile([P, BLOCKS], F32)
            nc.gpsimd.tensor_scalar(
                out=var_eps[:], in0=square_sum[:], scalar1=1.0 / CH, scalar2=LN_EPS, op0=ALU.mult, op1=ALU.add
            )
            inv_std = ahead.tile([P, BLOCKS], F32)
            nc.gpsimd.tensor_tensor(out=inv_std[:], in0=var_eps[:], in1=minus_half[:], op=ALU.pow)
            rstd[g] = inv_std

        def centre_and_gain(g):
            scaled = results.tile([P, BLOCKS, CH], F32)
            for s in range(BLOCKS):
                nc.vector.scalar_tensor_tensor(
                    out=scaled[:, s, :],
                    in0=resid[g][:, s, :],
                    scalar=neg_mean[g][:, s : s + 1],
                    in1=gain_shift[:, 0, :],
                    op0=ALU.add,
                    op1=ALU.mult,
                )
            normed[g] = scaled

        def scale_shift_store(g):
            scaled = normed[g]
            for s in range(BLOCKS):
                nc.vector.scalar_tensor_tensor(
                    out=scaled[:, s, :],
                    in0=scaled[:, s, :],
                    scalar=rstd[g][:, s : s + 1],
                    in1=gain_shift[:, 1, :],
                    op0=ALU.mult,
                    op1=ALU.add,
                )
            first = (g % GROUPS_IN_SLAB) * BLOCKS * CH
            nc.sync.dma_start(
                out=out_slabs[g // GROUPS_IN_SLAB][:, first : first + BLOCKS * CH],
                in_=scaled[:].rearrange("p s e -> p (s e)"),
            )

        done = set()

        def run(stage, g):
            if live(g) and (stage, g) not in done:
                done.add((stage, g))
                stage(g)

        def quantise_pair(k):
            y_due = live(k + 4) and (quantise_y, k + 4) not in done
            h_due = live(k + 1) and (quantise_hidden, k + 1) not in done
            if y_due and h_due:
                done.add((quantise_y, k + 4))
                done.add((quantise_hidden, k + 1))
                quantise_halves(k, 0, 1)
            run(quantise_y, k + 4)
            run(quantise_hidden, k + 1)

        def step(k):
            run(first_matmul, k + 3)
            run(residual, k)
            run(negate_mean, k - 1)
            run(gelu, k + 2)
            quantise_pair(k)
            run(second_matmul, k + 1)
            run(collect_tokens, k + 5)
            run(flip_tokens, k + 6)
            run(scale_shift_store, k - 3)
            run(add_second_bias, k + 2)
            run(regroup, k + 2)
            run(variance, k - 1)
            run(centre_and_gain, k - 1)

        w1_grouped = group_weight(w1_sb, "w1", psum_hid, (nc.vector.tensor_copy, nc.scalar.copy))
        w1_codes, w1_scales = quantise_weight(w1_grouped, "w1")
        run(flip_tokens, 0)
        run(collect_tokens, 0)
        run(quantise_y, 0)
        run(first_matmul, 0)
        run(gelu, 0)
        run(flip_tokens, 1)
        run(collect_tokens, 1)
        run(quantise_y, 1)
        w2_grouped = group_weight(w2_sb, "w2", psum_ffn, (nc.vector.tensor_copy, nc.vector.tensor_copy))
        run(first_matmul, 1)
        b2_bank = psum_ffn.tile([P, CH], F32, tag="bank")
        spread_vector(0, b2_bank[:])
        nc.vector.tensor_copy(out=b2_all[:], in_=b2_bank[:])
        run(add_second_bias, 0)
        w2_codes, w2_scales = quantise_weight(w2_grouped, "w2")
        run(regroup, 0)
        run(flip_tokens, 2)
        run(collect_tokens, 2)
        run(gelu, 1)
        run(flip_tokens, 3)
        run(quantise_hidden, 0)
        run(second_matmul, 0)
        run(quantise_y, 2)
        run(first_matmul, 2)
        spread_vector(1, gain_shift[:, 0, :])
        spread_vector(2, gain_shift[:, 1, :])
        run(residual, 0)
        run(regroup, 1)
        run(collect_tokens, 3)
        run(quantise_hidden, 1)
        run(second_matmul, 1)
        run(add_second_bias, 1)
        run(gelu, 2)
        run(quantise_y, 3)
        run(flip_tokens, 4)
        run(collect_tokens, 4)
        run(residual, 1)
        run(flip_tokens, 5)
        for k in range(N_GROUPS + 3):
            step(k)
